import numpy as np
import ml_dtypes


def mxq(x, axis, fmt="e4m3"):
    dtype, down = {"e4m3": (ml_dtypes.float8_e4m3fn, 7), "e5m2": (ml_dtypes.float8_e5m2, 14)}[fmt]
    v = np.moveaxis(np.asarray(x, np.float32).astype(ml_dtypes.bfloat16).astype(np.float64), axis, -1)
    blocks = v.reshape(v.shape[:-1] + (-1, 32))
    amax = np.abs(blocks).max(-1, keepdims=True)
    byte = np.maximum(np.where(amax > 0, np.frexp(amax)[1] - 1 + 127, 0) - down, 1)
    scale = np.exp2(byte - 127.0)
    codes = (blocks / scale).astype(np.float32).astype(dtype).astype(np.float64)
    return np.moveaxis((codes * scale).reshape(v.shape), -1, axis)


WIDE = False


def mx_kscale(k):
    if not WIDE:
        return np.ones(k)
    levels = np.array([10, -10, 5, -5, 0])
    a = np.random.permutation(np.resize(levels, k // 512 * 4)).reshape(k // 512, 4)
    idx = np.arange(k)
    return np.exp2(a[idx // 512, idx % 128 // 32])


BF16 = ml_dtypes.bfloat16


def bf(x):
    return np.asarray(x, np.float32).astype(BF16)


def f64(x):
    return np.asarray(x).astype(np.float64)


E2M1 = np.array([0.0, 0.5, 1.0, 1.5, 2.0, 3.0, 4.0, 6.0, -0.0, -0.5, -1.0, -1.5, -2.0, -3.0, -4.0, -6.0])


def pack_weight(w, fmt):
    k, n = w.shape
    w = f64(bf(w)).reshape(k // 32, 32, n)
    amax = np.abs(w).max(1)
    if fmt == "e4m3":
        byte = np.frexp(amax)[1] - 1 + 127 - 7
    else:
        mant, ex = np.frexp(amax / 6.0)
        byte = np.where(mant > 0.5, ex, ex - 1) + 127
    byte = np.clip(np.where(amax > 0, byte, 1), 1, 254)
    scaled = (w * np.exp2(127.0 - byte)[:, None, :]).reshape(k, n).astype(np.float32)
    by_word = np.ascontiguousarray(scaled.reshape(k // 512, 128, 4, n).transpose(0, 1, 3, 2))
    if fmt == "e4m3":
        words = by_word.astype(ml_dtypes.float8_e4m3fn).view(np.uint8)
    else:
        c = by_word.astype(ml_dtypes.float4_e2m1fn).view(np.uint8) & 0xF
        words = c[..., 0::2] | (c[..., 1::2] << 4)
    return np.ascontiguousarray(words), np.ascontiguousarray(byte.astype(np.uint8).reshape(k // 512, 16, n))


def unpack_weight(words, scales, fmt):
    g, p, n, _ = words.shape
    if fmt == "e4m3":
        vals = np.ascontiguousarray(words).view(ml_dtypes.float8_e4m3fn).astype(np.float64)
    else:
        nib = np.empty((g, p, n, 4), np.uint8)
        nib[..., 0::2] = words & 0xF
        nib[..., 1::2] = words >> 4
        vals = E2M1[nib]
    vals = vals * np.repeat(np.exp2(scales.astype(np.float64) - 127.0), 8, axis=1)[..., None]
    return vals.transpose(0, 1, 3, 2).reshape(g * 512, n)


N, B, T, C, R, O, NC, H, W = 4, 3072, 4, 128, 4, 512, 512, 16, 4
K = C * R
LEAKY_SLOPE = 0.01


def setup_inputs():
    s = mx_kscale(K)
    pooled = bf((0.65 + 0.3 * np.random.standard_normal((N, B, K))) * s)
    p = bf(0.65 + 0.5 * np.random.standard_normal((N, B, T, C)))
    stack = (4.0 / np.sqrt(K) * np.random.standard_normal((N, K, C)) - 4.0 / K) / s[None, :, None]
    words, scales = pack_weight(stack.reshape(-1, C), "e4m3")
    return {"pooled": pooled,
            "p": p,
            "Wout_words": words,
            "Wout_scales": scales}


def reference(pooled, p, Wout_words, Wout_scales):
    y = mxq(f64(pooled), 2, "e4m3") @ unpack_weight(Wout_words, Wout_scales, "e4m3").reshape(N, K, C)
    y = np.where(y >= 0, y, LEAKY_SLOPE * y)
    return np.max(f64(p) + y[:, :, None, :], axis=2)

@@ -1,0 +1,197 @@
+from contextlib import ExitStack
+
+import concourse.mybir as mybir
+from concourse.masks import make_identity
+
+F32 = mybir.dt.float32
+BF16 = mybir.dt.bfloat16
+I32 = mybir.dt.int32
+U32 = mybir.dt.uint32
+U8 = mybir.dt.uint8
+FP8X4 = mybir.dt.float8_e4m3fn_x4
+MAX = mybir.AluOpType.max
+ADD = mybir.AluOpType.add
+
+P = 128
+BINS = 4
+SAMPLES = 3072
+K = 512
+PACK = 4
+FRAMES = 4
+C = 128
+LEAKY_SLOPE = 0.01
+
+ROWS = SAMPLES // P
+CHUNK = 8
+PAIR = 2
+QUAD = 4
+LOAD_BUFS = 6
+AHEAD = LOAD_BUFS - 1
+RES_BUFS = 6
+
+FLOPS = 2 * BINS * SAMPLES * K * C
+
+
+def chunk_list():
+    chunks = [(n, j, CHUNK) for n in range(BINS) for j in range(0, ROWS, CHUNK)]
+    cut = []
+    for index, (n, j, size) in enumerate(chunks):
+        if index in (0, len(chunks) - 1):
+            cut.extend([(n, j, size // 2), (n, j + size // 2, size // 2)])
+        else:
+            cut.append((n, j, size))
+    return cut
+
+
+def tile_gmpahead_pa_t_e_kernel(tc, pooled, p, Wout_words, Wout_scales, out):
+    nc = tc.nc
+    with ExitStack() as ctx:
+        const = ctx.enter_context(tc.tile_pool(name="const", bufs=1))
+        x_pool = ctx.enter_context(tc.tile_pool(name="x", bufs=LOAD_BUFS))
+        f_pool = ctx.enter_context(tc.tile_pool(name="f", bufs=LOAD_BUFS))
+        mx_pool = ctx.enter_context(tc.tile_pool(name="mx", bufs=2))
+        work = ctx.enter_context(tc.tile_pool(name="work", bufs=3))
+        t_psum = ctx.enter_context(tc.psum_pool(name="t_psum", bufs=4))
+        y_psum = ctx.enter_context(tc.psum_pool(name="y_psum", bufs=4))
+        ctx.enter_context(tc.manual_schedule())
+
+        chunks = chunk_list()
+        n_chunks = len(chunks)
+        x_tiles = {}
+        f_tiles = {}
+        grouped_tiles = {}
+        code_tiles = {}
+        y_tiles = {}
+        small_tiles = {}
+        half_tiles = {}
+        top_tiles = {}
+        res_tiles = {}
+
+        def rows_of(dram, k):
+            n, first, size = chunks[k]
+            return dram[n].rearrange("(q j) w -> q j w", j=ROWS)[:, first : first + size, :]
+
+        def load_x(k):
+            x_tiles[k] = x_pool.tile([P, chunks[k][2], K], BF16, name="x")
+            nc.sync.dma_start(out=x_tiles[k][:], in_=rows_of(pooled, k))
+
+        def load_f(k):
+            f_tiles[k] = f_pool.tile([P, chunks[k][2], FRAMES * C], BF16, name="f")
+            nc.sync.dma_start(out=f_tiles[k][:], in_=rows_of(p.rearrange("n b t c -> n b (t c)"), k))
+
+        def transpose(k):
+            size = chunks[k][2]
+            words = x_tiles[k][:].bitcast(F32)
+            grouped_tiles[k] = mx_pool.tile([P, size, P, PACK], BF16, name="grouped", align_bytes=64)
+            grouped_words = grouped_tiles[k][:].bitcast(F32)
+            for j in range(0, size, PAIR):
+                xt = t_psum.tile([P, PAIR, 2, P], F32, name="xt")
+                for i in range(PAIR):
+                    for u in range(2):
+                        nc.tensor.transpose(xt[:, i, u, :], words[:, j + i, u : K // 2 : 2], ident[:])
+                nc.scalar.copy(
+                    out=grouped_words[:, j : j + PAIR, :, :],
+                    in_=xt[:].rearrange("r i u s -> r i s u"),
+                )
+
+        def quantise(k):
+            size = chunks[k][2]
+            codes = mx_pool.tile([P, size * P], U32, name="codes", align_bytes=64)
+            scales = mx_pool.tile([P, size * P], U8, name="scales", align_bytes=64)
+            nc.vector.quantize_mx(
+                out=codes[:].bitcast(FP8X4),
+                scales=scales[:],
+                in_=grouped_tiles[k][:].rearrange("r j s t -> r (j s t)"),
+            )
+            code_tiles[k] = (codes, scales)
+
+        def multiply(k):
+            n, first, size = chunks[k]
+            codes, scales = code_tiles[k]
+            y_tiles[k] = []
+            for j in range(0, size, QUAD):
+                y = y_psum.tile([P, QUAD, C], F32, name="y")
+                for i in range(QUAD):
+                    cols = slice((j + i) * P, (j + i + 1) * P)
+                    nc.tensor.matmul_mx(
+                        out=y[:, i, :],
+                        lhsT=codes[:, cols].bitcast(FP8X4),
+                        lhsT_scale=scales[:, cols],
+                        rhs=w_words[:, n, :].bitcast(FP8X4),
+                        rhs_scale=w_scales[:, n, :],
+                        start=True,
+                        stop=True,
+                    )
+                y_tiles[k].append(y)
+
+        def shrink(k):
+            small_tiles[k] = []
+            for y in y_tiles[k]:
+                small = work.tile([P, QUAD, C], F32, name="small", bufs=4)
+                nc.scalar.mul(out=small[:], in_=y[:], mul=LEAKY_SLOPE)
+                small_tiles[k].append(small)
+
+        def leaky(k):
+            size = chunks[k][2]
+            res_tiles[k] = work.tile([P, size, C], F32, name="res", bufs=RES_BUFS)
+            for h in range(size // QUAD):
+                nc.vector.tensor_tensor(
+                    out=res_tiles[k][:, h * QUAD : (h + 1) * QUAD, :],
+                    in0=y_tiles[k][h][:],
+                    in1=small_tiles[k][h][:],
+                    op=MAX,
+                )
+
+        def frames_first(k):
+            f = f_tiles[k][:].rearrange("q j (t c) -> q j t c", t=FRAMES)
+            half_tiles[k] = work.tile([P, chunks[k][2], 2, C], BF16, name="half", bufs=2)
+            nc.vector.tensor_tensor(out=half_tiles[k][:], in0=f[:, :, 0:2, :], in1=f[:, :, 2:4, :], op=MAX)
+
+        def frames_second(k):
+            half = half_tiles[k]
+            top_tiles[k] = work.tile([P, chunks[k][2], C], BF16, name="top", bufs=4)
+            nc.vector.tensor_tensor(out=top_tiles[k][:], in0=half[:, :, 0, :], in1=half[:, :, 1, :], op=MAX)
+
+        def finish(k):
+            nc.vector.tensor_tensor(out=res_tiles[k][:], in0=res_tiles[k][:], in1=top_tiles[k][:], op=ADD)
+            nc.scalar.dma_start(out=rows_of(out, k), in_=res_tiles[k][:])
+
+        ident = const.tile([P, P], F32, name="ident")
+        make_identity(nc, ident[:])
+        w_words = const.tile([P, BINS, C * PACK], U8, name="w_words", align_bytes=64)
+        w_scales = const.tile([P, BINS, C], U8, name="w_scales", align_bytes=64)
+        nc.vector.memset(w_scales[:].bitcast(I32), 0)
+
+        load_x(0)
+        load_f(0)
+        nc.sync.dma_start(
+            out=w_words[:].bitcast(I32),
+            in_=Wout_words.rearrange("g r c t -> r g (c t)").bitcast(I32),
+        )
+        for quadrant in range(4):
+            nc.sync.dma_start(
+                out=w_scales[32 * quadrant : 32 * quadrant + 4].bitcast(I32),
+                in_=Wout_scales[:, 4 * quadrant : 4 * quadrant + 4, :].rearrange("g q c -> q g c").bitcast(I32),
+            )
+        for k in range(1, AHEAD):
+            load_x(k)
+            load_f(k)
+
+        for k in range(n_chunks + 2):
+            if k + AHEAD < n_chunks:
+                load_x(k + AHEAD)
+                load_f(k + AHEAD)
+            if k < n_chunks:
+                transpose(k)
+            if 1 <= k <= n_chunks:
+                multiply(k - 1)
+                shrink(k - 1)
+            if k >= 2:
+                leaky(k - 2)
+            if k < n_chunks:
+                frames_first(k)
+            if k >= 2:
+                finish(k - 2)
+            if k < n_chunks:
+                frames_second(k)
+                quantise(k)

@@ -11,6 +11,7 @@ U8 = mybir.dt.uint8
 FP8X4 = mybir.dt.float8_e4m3fn_x4
 MAX = mybir.AluOpType.max
 ADD = mybir.AluOpType.add
+RELU = mybir.ActivationFunctionType.Relu
 
 P = 128
 BINS = 4
@@ -28,6 +29,7 @@ QUAD = 4
 LOAD_BUFS = 6
 AHEAD = LOAD_BUFS - 1
 RES_BUFS = 6
+TURN_EVERY = 2
 
 FLOPS = 2 * BINS * SAMPLES * K * C
 
@@ -51,8 +53,9 @@ def tile_gmpahead_pa_t_e_kernel(tc, pooled, p, Wout_words, Wout_scales, out):
         f_pool = ctx.enter_context(tc.tile_pool(name="f", bufs=LOAD_BUFS))
         mx_pool = ctx.enter_context(tc.tile_pool(name="mx", bufs=2))
         work = ctx.enter_context(tc.tile_pool(name="work", bufs=3))
-        t_psum = ctx.enter_context(tc.psum_pool(name="t_psum", bufs=4))
-        y_psum = ctx.enter_context(tc.psum_pool(name="y_psum", bufs=4))
+        t_psum = ctx.enter_context(tc.psum_pool(name="t_psum", bufs=3))
+        y_psum = ctx.enter_context(tc.psum_pool(name="y_psum", bufs=3))
+        turn_psum = ctx.enter_context(tc.psum_pool(name="turn_psum", bufs=1))
         ctx.enter_context(tc.manual_schedule())
 
         chunks = chunk_list()
@@ -66,6 +69,12 @@ def tile_gmpahead_pa_t_e_kernel(tc, pooled, p, Wout_words, Wout_scales, out):
         half_tiles = {}
         top_tiles = {}
         res_tiles = {}
+        turned_y = {}
+        part_tiles = {}
+
+        def plain_quads(k):
+            size = chunks[k][2]
+            return size - QUAD if size == CHUNK and k % TURN_EVERY == 0 else size
 
         def rows_of(dram, k):
             n, first, size = chunks[k]
@@ -109,7 +118,7 @@ def tile_gmpahead_pa_t_e_kernel(tc, pooled, p, Wout_words, Wout_scales, out):
             n, first, size = chunks[k]
             codes, scales = code_tiles[k]
             y_tiles[k] = []
-            for j in range(0, size, QUAD):
+            for j in range(0, plain_quads(k), QUAD):
                 y = y_psum.tile([P, QUAD, C], F32, name="y")
                 for i in range(QUAD):
                     cols = slice((j + i) * P, (j + i + 1) * P)
@@ -123,6 +132,46 @@ def tile_gmpahead_pa_t_e_kernel(tc, pooled, p, Wout_words, Wout_scales, out):
                         stop=True,
                     )
                 y_tiles[k].append(y)
+            if plain_quads(k) < size:
+                turned_y[k] = turn_psum.tile([P, QUAD * P], F32, name="turned_y")
+                cols = slice(plain_quads(k) * P, size * P)
+                nc.tensor.matmul_mx(
+                    out=turned_y[k][:],
+                    lhsT=w_words[:, n, :].bitcast(FP8X4),
+                    lhsT_scale=w_scales[:, n, :],
+                    rhs=codes[:, cols].bitcast(FP8X4),
+                    rhs_scale=scales[:, cols],
+                    start=True,
+                    stop=True,
+                )
+
+        def turn_back(k):
+            first = plain_quads(k)
+            if first == chunks[k][2]:
+                return
+            bent, straight = part_tiles[k]
+            feat = turn_psum.tile([P, QUAD, C], F32, name="feat")
+            nc.tensor.matmul(
+                out=feat[:].rearrange("q j c -> q (j c)"),
+                lhsT=ident_bf[:],
+                rhs=top_tiles[k][:, first : first + QUAD, :].rearrange("q j c -> q (j c)"),
+                start=True,
+                stop=False,
+            )
+            for j in range(QUAD):
+                cols = slice(j * P, (j + 1) * P)
+                nc.tensor.matmul(
+                    out=feat[:, j, :], lhsT=bent[:, cols], rhs=ident[:], is_transpose=True, start=False, stop=False
+                )
+                nc.tensor.matmul(
+                    out=feat[:, j, :],
+                    lhsT=straight[:, cols],
+                    rhs=ident[:],
+                    is_transpose=True,
+                    start=False,
+                    stop=(j == QUAD - 1),
+                )
+            nc.scalar.copy(out=res_tiles[k][:, first : first + QUAD, :], in_=feat[:])
 
         def shrink(k):
             small_tiles[k] = []
@@ -130,11 +179,15 @@ def tile_gmpahead_pa_t_e_kernel(tc, pooled, p, Wout_words, Wout_scales, out):
                 small = work.tile([P, QUAD, C], F32, name="small", bufs=4)
                 nc.scalar.mul(out=small[:], in_=y[:], mul=LEAKY_SLOPE)
                 small_tiles[k].append(small)
+            if k in turned_y:
+                bent = work.tile([P, QUAD * P], F32, name="bent", bufs=2)
+                straight = work.tile([P, QUAD * P], F32, name="straight", bufs=2)
+                nc.scalar.activation(out=bent[:], in_=turned_y[k][:], func=RELU, scale=1.0 - LEAKY_SLOPE)
+                nc.scalar.mul(out=straight[:], in_=turned_y[k][:], mul=LEAKY_SLOPE)
+                part_tiles[k] = (bent, straight)
 
         def leaky(k):
-            size = chunks[k][2]
-            res_tiles[k] = work.tile([P, size, C], F32, name="res", bufs=RES_BUFS)
-            for h in range(size // QUAD):
+            for h in range(plain_quads(k) // QUAD):
                 nc.vector.tensor_tensor(
                     out=res_tiles[k][:, h * QUAD : (h + 1) * QUAD, :],
                     in0=y_tiles[k][h][:],
@@ -153,11 +206,16 @@ def tile_gmpahead_pa_t_e_kernel(tc, pooled, p, Wout_words, Wout_scales, out):
             nc.vector.tensor_tensor(out=top_tiles[k][:], in0=half[:, :, 0, :], in1=half[:, :, 1, :], op=MAX)
 
         def finish(k):
-            nc.vector.tensor_tensor(out=res_tiles[k][:], in0=res_tiles[k][:], in1=top_tiles[k][:], op=ADD)
+            mine = slice(0, plain_quads(k))
+            nc.vector.tensor_tensor(
+                out=res_tiles[k][:, mine, :], in0=res_tiles[k][:, mine, :], in1=top_tiles[k][:, mine, :], op=ADD
+            )
             nc.scalar.dma_start(out=rows_of(out, k), in_=res_tiles[k][:])
 
         ident = const.tile([P, P], F32, name="ident")
         make_identity(nc, ident[:])
+        ident_bf = const.tile([P, P], BF16, name="ident_bf")
+        make_identity(nc, ident_bf[:])
         w_words = const.tile([P, BINS, C * PACK], U8, name="w_words", align_bytes=64)
         w_scales = const.tile([P, BINS, C], U8, name="w_scales", align_bytes=64)
         nc.vector.memset(w_scales[:].bitcast(I32), 0)
@@ -183,11 +241,13 @@ def tile_gmpahead_pa_t_e_kernel(tc, pooled, p, Wout_words, Wout_scales, out):
                 load_f(k + AHEAD)
             if k < n_chunks:
                 transpose(k)
+            if k >= 2:
+                res_tiles[k - 2] = work.tile([P, chunks[k - 2][2], C], F32, name="res", bufs=RES_BUFS)
+                turn_back(k - 2)
+                leaky(k - 2)
             if 1 <= k <= n_chunks:
                 multiply(k - 1)
                 shrink(k - 1)
-            if k >= 2:
-                leaky(k - 2)
             if k < n_chunks:
                 frames_first(k)
             if k >= 2:

@@ -29,7 +29,7 @@ QUAD = 4
 LOAD_BUFS = 6
 AHEAD = LOAD_BUFS - 1
 RES_BUFS = 6
-TURN_EVERY = 2
+TURNED = 9
 
 FLOPS = 2 * BINS * SAMPLES * K * C
 
@@ -74,7 +74,7 @@ def tile_gmpahead_pa_t_e_kernel(tc, pooled, p, Wout_words, Wout_scales, out):
 
         def plain_quads(k):
             size = chunks[k][2]
-            return size - QUAD if size == CHUNK and k % TURN_EVERY == 0 else size
+            return size - QUAD if size == CHUNK and k < 2 + TURNED else size
 
         def rows_of(dram, k):
             n, first, size = chunks[k]
@@ -180,8 +180,8 @@ def tile_gmpahead_pa_t_e_kernel(tc, pooled, p, Wout_words, Wout_scales, out):
                 nc.scalar.mul(out=small[:], in_=y[:], mul=LEAKY_SLOPE)
                 small_tiles[k].append(small)
             if k in turned_y:
-                bent = work.tile([P, QUAD * P], F32, name="bent", bufs=2)
-                straight = work.tile([P, QUAD * P], F32, name="straight", bufs=2)
+                bent = work.tile([P, QUAD * P], F32, name="bent", bufs=3)
+                straight = work.tile([P, QUAD * P], F32, name="straight", bufs=3)
                 nc.scalar.activation(out=bent[:], in_=turned_y[k][:], func=RELU, scale=1.0 - LEAKY_SLOPE)
                 nc.scalar.mul(out=straight[:], in_=turned_y[k][:], mul=LEAKY_SLOPE)
                 part_tiles[k] = (bent, straight)
@@ -221,7 +221,6 @@ def tile_gmpahead_pa_t_e_kernel(tc, pooled, p, Wout_words, Wout_scales, out):
         nc.vector.memset(w_scales[:].bitcast(I32), 0)
 
         load_x(0)
-        load_f(0)
         nc.sync.dma_start(
             out=w_words[:].bitcast(I32),
             in_=Wout_words.rearrange("g r c t -> r g (c t)").bitcast(I32),
@@ -233,25 +232,29 @@ def tile_gmpahead_pa_t_e_kernel(tc, pooled, p, Wout_words, Wout_scales, out):
             )
         for k in range(1, AHEAD):
             load_x(k)
-            load_f(k)
+            if k >= 2:
+                load_f(k - 2)
 
-        for k in range(n_chunks + 2):
+        for k in range(n_chunks + 3):
             if k + AHEAD < n_chunks:
                 load_x(k + AHEAD)
-                load_f(k + AHEAD)
+            if k + AHEAD - 2 < n_chunks:
+                load_f(k + AHEAD - 2)
             if k < n_chunks:
                 transpose(k)
-            if k >= 2:
+            if k >= 3:
+                turn_back(k - 3)
+            if 2 <= k <= n_chunks + 1:
                 res_tiles[k - 2] = work.tile([P, chunks[k - 2][2], C], F32, name="res", bufs=RES_BUFS)
-                turn_back(k - 2)
                 leaky(k - 2)
             if 1 <= k <= n_chunks:
                 multiply(k - 1)
                 shrink(k - 1)
+            if 2 <= k <= n_chunks + 1:
+                frames_first(k - 2)
+            if k >= 3:
+                finish(k - 3)
+            if 2 <= k <= n_chunks + 1:
+                frames_second(k - 2)
             if k < n_chunks:
-                frames_first(k)
-            if k >= 2:
-                finish(k - 2)
-            if k < n_chunks:
-                frames_second(k)
                 quantise(k)

@@ -29,7 +29,7 @@ QUAD = 4
 LOAD_BUFS = 6
 AHEAD = LOAD_BUFS - 1
 RES_BUFS = 6
-TURNED = 9
+TURN_EVERY = 2
 
 FLOPS = 2 * BINS * SAMPLES * K * C
 
@@ -74,7 +74,7 @@ def tile_gmpahead_pa_t_e_kernel(tc, pooled, p, Wout_words, Wout_scales, out):
 
         def plain_quads(k):
             size = chunks[k][2]
-            return size - QUAD if size == CHUNK and k < 2 + TURNED else size
+            return size - QUAD if size == CHUNK and k % TURN_EVERY == 0 else size
 
         def rows_of(dram, k):
             n, first, size = chunks[k]
@@ -242,14 +242,14 @@ def tile_gmpahead_pa_t_e_kernel(tc, pooled, p, Wout_words, Wout_scales, out):
                 load_f(k + AHEAD - 2)
             if k < n_chunks:
                 transpose(k)
-            if k >= 3:
-                turn_back(k - 3)
             if 2 <= k <= n_chunks + 1:
                 res_tiles[k - 2] = work.tile([P, chunks[k - 2][2], C], F32, name="res", bufs=RES_BUFS)
                 leaky(k - 2)
             if 1 <= k <= n_chunks:
                 multiply(k - 1)
                 shrink(k - 1)
+            if k >= 3:
+                turn_back(k - 3)
             if 2 <= k <= n_chunks + 1:
                 frames_first(k - 2)
             if k >= 3:

@@ -30,6 +30,7 @@ LOAD_BUFS = 6
 AHEAD = LOAD_BUFS - 1
 RES_BUFS = 6
 TURN_EVERY = 2
+TURN_LAST = 3
 
 FLOPS = 2 * BINS * SAMPLES * K * C
 
@@ -55,7 +56,7 @@ def tile_gmpahead_pa_t_e_kernel(tc, pooled, p, Wout_words, Wout_scales, out):
         work = ctx.enter_context(tc.tile_pool(name="work", bufs=3))
         t_psum = ctx.enter_context(tc.psum_pool(name="t_psum", bufs=3))
         y_psum = ctx.enter_context(tc.psum_pool(name="y_psum", bufs=3))
-        turn_psum = ctx.enter_context(tc.psum_pool(name="turn_psum", bufs=1))
+        turn_psum = ctx.enter_context(tc.psum_pool(name="turn_psum", bufs=2))
         ctx.enter_context(tc.manual_schedule())
 
         chunks = chunk_list()
@@ -71,9 +72,15 @@ def tile_gmpahead_pa_t_e_kernel(tc, pooled, p, Wout_words, Wout_scales, out):
         res_tiles = {}
         turned_y = {}
         part_tiles = {}
+        leaky_tiles = {}
+
+        def at_end(k):
+            return k >= n_chunks - TURN_LAST
 
         def plain_quads(k):
             size = chunks[k][2]
+            if at_end(k):
+                return 0
             return size - QUAD if size == CHUNK and k % TURN_EVERY == 0 else size
 
         def rows_of(dram, k):
@@ -132,11 +139,12 @@ def tile_gmpahead_pa_t_e_kernel(tc, pooled, p, Wout_words, Wout_scales, out):
                         stop=True,
                     )
                 y_tiles[k].append(y)
-            if plain_quads(k) < size:
-                turned_y[k] = turn_psum.tile([P, QUAD * P], F32, name="turned_y")
-                cols = slice(plain_quads(k) * P, size * P)
+            turned_y[k] = []
+            for j in range(plain_quads(k), size, QUAD):
+                y = y_psum.tile([P, QUAD * P], F32, name="y")
+                cols = slice(j * P, (j + QUAD) * P)
                 nc.tensor.matmul_mx(
-                    out=turned_y[k][:],
+                    out=y[:],
                     lhsT=w_words[:, n, :].bitcast(FP8X4),
                     lhsT_scale=w_scales[:, n, :],
                     rhs=codes[:, cols].bitcast(FP8X4),
@@ -144,34 +152,47 @@ def tile_gmpahead_pa_t_e_kernel(tc, pooled, p, Wout_words, Wout_scales, out):
                     start=True,
                     stop=True,
                 )
+                turned_y[k].append(y)
 
         def turn_back(k):
-            first = plain_quads(k)
-            if first == chunks[k][2]:
+            if at_end(k):
+                leaky_tiles[k] = []
+                for bent, straight in part_tiles[k]:
+                    turned_back = t_psum.tile([P, QUAD, C], F32, name="xt")
+                    for j in range(QUAD):
+                        cols = slice(j * P, (j + 1) * P)
+                        nc.tensor.matmul(
+                            out=turned_back[:, j, :], lhsT=bent[:, cols], rhs=ident[:], is_transpose=True, start=True, stop=False
+                        )
+                        nc.tensor.matmul(
+                            out=turned_back[:, j, :], lhsT=straight[:, cols], rhs=ident[:], is_transpose=True, start=False, stop=True
+                        )
+                    leaky_tiles[k].append(turned_back)
                 return
-            bent, straight = part_tiles[k]
-            feat = turn_psum.tile([P, QUAD, C], F32, name="feat")
-            nc.tensor.matmul(
-                out=feat[:].rearrange("q j c -> q (j c)"),
-                lhsT=ident_bf[:],
-                rhs=top_tiles[k][:, first : first + QUAD, :].rearrange("q j c -> q (j c)"),
-                start=True,
-                stop=False,
-            )
-            for j in range(QUAD):
-                cols = slice(j * P, (j + 1) * P)
+            for index, (bent, straight) in enumerate(part_tiles[k]):
+                first = plain_quads(k) + index * QUAD
+                feat = turn_psum.tile([P, QUAD, C], F32, name="feat")
                 nc.tensor.matmul(
-                    out=feat[:, j, :], lhsT=bent[:, cols], rhs=ident[:], is_transpose=True, start=False, stop=False
+                    out=feat[:].rearrange("q j c -> q (j c)"),
+                    lhsT=ident_bf[:],
+                    rhs=top_tiles[k][:, first : first + QUAD, :].rearrange("q j c -> q (j c)"),
+                    start=True,
+                    stop=False,
                 )
-                nc.tensor.matmul(
-                    out=feat[:, j, :],
-                    lhsT=straight[:, cols],
-                    rhs=ident[:],
-                    is_transpose=True,
-                    start=False,
-                    stop=(j == QUAD - 1),
-                )
-            nc.scalar.copy(out=res_tiles[k][:, first : first + QUAD, :], in_=feat[:])
+                for j in range(QUAD):
+                    cols = slice(j * P, (j + 1) * P)
+                    nc.tensor.matmul(
+                        out=feat[:, j, :], lhsT=bent[:, cols], rhs=ident[:], is_transpose=True, start=False, stop=False
+                    )
+                    nc.tensor.matmul(
+                        out=feat[:, j, :],
+                        lhsT=straight[:, cols],
+                        rhs=ident[:],
+                        is_transpose=True,
+                        start=False,
+                        stop=(j == QUAD - 1),
+                    )
+                nc.scalar.copy(out=res_tiles[k][:, first : first + QUAD, :], in_=feat[:])
 
         def shrink(k):
             small_tiles[k] = []
@@ -179,12 +200,13 @@ def tile_gmpahead_pa_t_e_kernel(tc, pooled, p, Wout_words, Wout_scales, out):
                 small = work.tile([P, QUAD, C], F32, name="small", bufs=4)
                 nc.scalar.mul(out=small[:], in_=y[:], mul=LEAKY_SLOPE)
                 small_tiles[k].append(small)
-            if k in turned_y:
-                bent = work.tile([P, QUAD * P], F32, name="bent", bufs=3)
-                straight = work.tile([P, QUAD * P], F32, name="straight", bufs=3)
-                nc.scalar.activation(out=bent[:], in_=turned_y[k][:], func=RELU, scale=1.0 - LEAKY_SLOPE)
-                nc.scalar.mul(out=straight[:], in_=turned_y[k][:], mul=LEAKY_SLOPE)
-                part_tiles[k] = (bent, straight)
+            part_tiles[k] = []
+            for y in turned_y[k]:
+                bent = work.tile([P, QUAD * P], F32, name="bent", bufs=4)
+                straight = work.tile([P, QUAD * P], F32, name="straight", bufs=4)
+                nc.scalar.activation(out=bent[:], in_=y[:], func=RELU, scale=1.0 - LEAKY_SLOPE)
+                nc.scalar.mul(out=straight[:], in_=y[:], mul=LEAKY_SLOPE)
+                part_tiles[k].append((bent, straight))
 
         def leaky(k):
             for h in range(plain_quads(k) // QUAD):
@@ -207,10 +229,17 @@ def tile_gmpahead_pa_t_e_kernel(tc, pooled, p, Wout_words, Wout_scales, out):
 
         def finish(k):
             mine = slice(0, plain_quads(k))
-            nc.vector.tensor_tensor(
-                out=res_tiles[k][:, mine, :], in0=res_tiles[k][:, mine, :], in1=top_tiles[k][:, mine, :], op=ADD
-            )
-            nc.scalar.dma_start(out=rows_of(out, k), in_=res_tiles[k][:])
+            for index, turned_back in enumerate(leaky_tiles.get(k, [])):
+                quad = slice(index * QUAD, (index + 1) * QUAD)
+                nc.vector.tensor_tensor(
+                    out=res_tiles[k][:, quad, :], in0=turned_back[:], in1=top_tiles[k][:, quad, :], op=ADD
+                )
+            if plain_quads(k) > 0:
+                nc.vector.tensor_tensor(
+                    out=res_tiles[k][:, mine, :], in0=res_tiles[k][:, mine, :], in1=top_tiles[k][:, mine, :], op=ADD
+                )
+            queue = nc.sync if len(x_tiles) + len(f_tiles) == 2 * n_chunks else nc.scalar
+            queue.dma_start(out=rows_of(out, k), in_=res_tiles[k][:])
 
         ident = const.tile([P, P], F32, name="ident")
         make_identity(nc, ident[:])
@@ -248,8 +277,10 @@ def tile_gmpahead_pa_t_e_kernel(tc, pooled, p, Wout_words, Wout_scales, out):
             if 1 <= k <= n_chunks:
                 multiply(k - 1)
                 shrink(k - 1)
-            if k >= 3:
+            if k >= 3 and not at_end(k - 3):
                 turn_back(k - 3)
+            if 2 <= k <= n_chunks + 1 and at_end(k - 2):
+                turn_back(k - 2)
             if 2 <= k <= n_chunks + 1:
                 frames_first(k - 2)
             if k >= 3:

@@ -28,7 +28,7 @@ PAIR = 2
 QUAD = 4
 LOAD_BUFS = 6
 AHEAD = LOAD_BUFS - 1
-RES_BUFS = 6
+RES_BUFS = 8
 TURN_EVERY = 2
 TURN_LAST = 3
 
@@ -238,8 +238,7 @@ def tile_gmpahead_pa_t_e_kernel(tc, pooled, p, Wout_words, Wout_scales, out):
                 nc.vector.tensor_tensor(
                     out=res_tiles[k][:, mine, :], in0=res_tiles[k][:, mine, :], in1=top_tiles[k][:, mine, :], op=ADD
                 )
-            queue = nc.sync if len(x_tiles) + len(f_tiles) == 2 * n_chunks else nc.scalar
-            queue.dma_start(out=rows_of(out, k), in_=res_tiles[k][:])
+            nc.sync.dma_start(out=rows_of(out, k), in_=res_tiles[k][:])
 
         ident = const.tile([P, P], F32, name="ident")
         make_identity(nc, ident[:])

@@ -29,7 +29,7 @@ QUAD = 4
 LOAD_BUFS = 6
 AHEAD = LOAD_BUFS - 1
 RES_BUFS = 8
-TURN_EVERY = 2
+TURNED = (2, 4, 6, 8, 9, 10)
 TURN_LAST = 3
 
 FLOPS = 2 * BINS * SAMPLES * K * C
@@ -81,11 +81,11 @@ def tile_gmpahead_pa_t_e_kernel(tc, pooled, p, Wout_words, Wout_scales, out):
             size = chunks[k][2]
             if at_end(k):
                 return 0
-            return size - QUAD if size == CHUNK and k % TURN_EVERY == 0 else size
+            return size - QUAD if size == CHUNK and k in TURNED else size
 
         def rows_of(dram, k):
             n, first, size = chunks[k]
-            return dram[n].rearrange("(q j) w -> q j w", j=ROWS)[:, first : first + size, :]
+            return dram[n][first * P : (first + size) * P, :].rearrange("(q j) w -> q j w", j=size)
 
         def load_x(k):
             x_tiles[k] = x_pool.tile([P, chunks[k][2], K], BF16, name="x")

@@ -26,9 +26,13 @@ ROWS = SAMPLES // P
 CHUNK = 8
 PAIR = 2
 QUAD = 4
-LOAD_BUFS = 6
-AHEAD = LOAD_BUFS - 1
-RES_BUFS = 8
+X_BUFS = 5
+P_BUFS = 4
+AHEAD = 5
+P_CUTS = ((4, 4, 16), (8, 16), (8, 16), (8, 8, 4, 4))
+OUT_CUTS = ((8, 16), (24,), (24,), (8, 8, 4, 4))
+LONG_RES_BUFS = 3
+SHORT_RES_BUFS = 4
 TURNED = (2, 4, 6, 8, 9, 10)
 TURN_LAST = 3
 
@@ -46,12 +50,16 @@ def chunk_list():
     return cut
 
 
+def pieces(cuts):
+    return [(n, sum(cut[:i]), size) for n, cut in enumerate(cuts) for i, size in enumerate(cut)]
+
+
 def tile_gmpahead_pa_t_e_kernel(tc, pooled, p, Wout_words, Wout_scales, out):
     nc = tc.nc
     with ExitStack() as ctx:
         const = ctx.enter_context(tc.tile_pool(name="const", bufs=1))
-        x_pool = ctx.enter_context(tc.tile_pool(name="x", bufs=LOAD_BUFS))
-        f_pool = ctx.enter_context(tc.tile_pool(name="f", bufs=LOAD_BUFS))
+        x_pool = ctx.enter_context(tc.tile_pool(name="x", bufs=X_BUFS))
+        f_pool = ctx.enter_context(tc.tile_pool(name="f", bufs=P_BUFS))
         mx_pool = ctx.enter_context(tc.tile_pool(name="mx", bufs=2))
         work = ctx.enter_context(tc.tile_pool(name="work", bufs=3))
         t_psum = ctx.enter_context(tc.psum_pool(name="t_psum", bufs=3))
@@ -61,6 +69,8 @@ def tile_gmpahead_pa_t_e_kernel(tc, pooled, p, Wout_words, Wout_scales, out):
 
         chunks = chunk_list()
         n_chunks = len(chunks)
+        p_pieces = pieces(P_CUTS)
+        out_pieces = pieces(OUT_CUTS)
         x_tiles = {}
         f_tiles = {}
         grouped_tiles = {}
@@ -83,17 +93,35 @@ def tile_gmpahead_pa_t_e_kernel(tc, pooled, p, Wout_words, Wout_scales, out):
                 return 0
             return size - QUAD if size == CHUNK and k in TURNED else size
 
-        def rows_of(dram, k):
-            n, first, size = chunks[k]
-            return dram[n][first * P : (first + size) * P, :].rearrange("(q j) w -> q j w", j=size)
+        def rows_of(dram, piece):
+            n, first, size = piece
+            return dram[n].rearrange("(q j) w -> q j w", j=ROWS)[:, first : first + size, :]
 
         def load_x(k):
             x_tiles[k] = x_pool.tile([P, chunks[k][2], K], BF16, name="x")
-            nc.sync.dma_start(out=x_tiles[k][:], in_=rows_of(pooled, k))
+            nc.sync.dma_start(out=x_tiles[k][:], in_=rows_of(pooled, chunks[k]))
+
+        def place(k, longer):
+            n, first, size = chunks[k]
+            for i, (piece_n, piece_first, piece_size) in enumerate(longer):
+                if piece_n == n and piece_first <= first < piece_first + piece_size:
+                    return i, slice(first - piece_first, first - piece_first + size)
 
         def load_f(k):
-            f_tiles[k] = f_pool.tile([P, chunks[k][2], FRAMES * C], BF16, name="f")
-            nc.sync.dma_start(out=f_tiles[k][:], in_=rows_of(p.rearrange("n b t c -> n b (t c)"), k))
+            i, tiles = place(k, p_pieces)
+            if tiles.start == 0:
+                f_tiles[i] = f_pool.tile([P, p_pieces[i][2], FRAMES * C], BF16, name="f")
+                nc.sync.dma_start(out=f_tiles[i][:], in_=rows_of(p.rearrange("n b t c -> n b (t c)"), p_pieces[i]))
+
+        def result(k):
+            i, tiles = place(k, out_pieces)
+            if i not in res_tiles:
+                size = out_pieces[i][2]
+                if size > CHUNK:
+                    res_tiles[i] = work.tile([P, size, C], F32, name="long_res", bufs=LONG_RES_BUFS)
+                else:
+                    res_tiles[i] = work.tile([P, size, C], F32, name="short_res", bufs=SHORT_RES_BUFS)
+            return res_tiles[i][:, tiles, :]
 
         def transpose(k):
             size = chunks[k][2]
@@ -192,7 +220,7 @@ def tile_gmpahead_pa_t_e_kernel(tc, pooled, p, Wout_words, Wout_scales, out):
                         start=False,
                         stop=(j == QUAD - 1),
                     )
-                nc.scalar.copy(out=res_tiles[k][:, first : first + QUAD, :], in_=feat[:])
+                nc.scalar.copy(out=result(k)[:, first : first + QUAD, :], in_=feat[:])
 
         def shrink(k):
             small_tiles[k] = []
@@ -211,14 +239,15 @@ def tile_gmpahead_pa_t_e_kernel(tc, pooled, p, Wout_words, Wout_scales, out):
         def leaky(k):
             for h in range(plain_quads(k) // QUAD):
                 nc.vector.tensor_tensor(
-                    out=res_tiles[k][:, h * QUAD : (h + 1) * QUAD, :],
+                    out=result(k)[:, h * QUAD : (h + 1) * QUAD, :],
                     in0=y_tiles[k][h][:],
                     in1=small_tiles[k][h][:],
                     op=MAX,
                 )
 
         def frames_first(k):
-            f = f_tiles[k][:].rearrange("q j (t c) -> q j t c", t=FRAMES)
+            i, tiles = place(k, p_pieces)
+            f = f_tiles[i][:, tiles, :].rearrange("q j (t c) -> q j t c", t=FRAMES)
             half_tiles[k] = work.tile([P, chunks[k][2], 2, C], BF16, name="half", bufs=2)
             nc.vector.tensor_tensor(out=half_tiles[k][:], in0=f[:, :, 0:2, :], in1=f[:, :, 2:4, :], op=MAX)
 
@@ -232,13 +261,15 @@ def tile_gmpahead_pa_t_e_kernel(tc, pooled, p, Wout_words, Wout_scales, out):
             for index, turned_back in enumerate(leaky_tiles.get(k, [])):
                 quad = slice(index * QUAD, (index + 1) * QUAD)
                 nc.vector.tensor_tensor(
-                    out=res_tiles[k][:, quad, :], in0=turned_back[:], in1=top_tiles[k][:, quad, :], op=ADD
+                    out=result(k)[:, quad, :], in0=turned_back[:], in1=top_tiles[k][:, quad, :], op=ADD
                 )
             if plain_quads(k) > 0:
                 nc.vector.tensor_tensor(
-                    out=res_tiles[k][:, mine, :], in0=res_tiles[k][:, mine, :], in1=top_tiles[k][:, mine, :], op=ADD
+                    out=result(k)[:, mine, :], in0=result(k)[:, mine, :], in1=top_tiles[k][:, mine, :], op=ADD
                 )
-            nc.sync.dma_start(out=rows_of(out, k), in_=res_tiles[k][:])
+            i, tiles = place(k, out_pieces)
+            if tiles.stop == out_pieces[i][2]:
+                nc.sync.dma_start(out=rows_of(out, out_pieces[i]), in_=res_tiles[i][:])
 
         ident = const.tile([P, P], F32, name="ident")
         make_identity(nc, ident[:])
@@ -271,7 +302,6 @@ def tile_gmpahead_pa_t_e_kernel(tc, pooled, p, Wout_words, Wout_scales, out):
             if k < n_chunks:
                 transpose(k)
             if 2 <= k <= n_chunks + 1:
-                res_tiles[k - 2] = work.tile([P, chunks[k - 2][2], C], F32, name="res", bufs=RES_BUFS)
                 leaky(k - 2)
             if 1 <= k <= n_chunks:
                 multiply(k - 1)

@@ -29,12 +29,12 @@ QUAD = 4
 X_BUFS = 5
 P_BUFS = 4
 AHEAD = 5
-P_CUTS = ((4, 4, 16), (8, 16), (8, 16), (8, 8, 4, 4))
-OUT_CUTS = ((8, 16), (24,), (24,), (8, 8, 4, 4))
+P_CUTS = ((8, 16), (8, 16), (8, 16), (8, 8, 8))
+OUT_CUTS = ((24,), (24,), (24,), (8, 8, 8))
 LONG_RES_BUFS = 3
 SHORT_RES_BUFS = 4
 TURNED = (2, 4, 6, 8, 9, 10)
-TURN_LAST = 3
+TURN_LAST = 2
 
 FLOPS = 2 * BINS * SAMPLES * K * C
 
@@ -43,7 +43,7 @@ def chunk_list():
     chunks = [(n, j, CHUNK) for n in range(BINS) for j in range(0, ROWS, CHUNK)]
     cut = []
     for index, (n, j, size) in enumerate(chunks):
-        if index in (0, len(chunks) - 1):
+        if index == 0:
             cut.extend([(n, j, size // 2), (n, j + size // 2, size // 2)])
         else:
             cut.append((n, j, size))

@@ -29,25 +29,18 @@ QUAD = 4
 X_BUFS = 5
 P_BUFS = 4
 AHEAD = 5
-P_CUTS = ((8, 16), (8, 16), (8, 16), (8, 8, 8))
+P_CUTS = ((8, 16), (8, 16), (8, 16), (8, 16))
 OUT_CUTS = ((24,), (24,), (24,), (8, 8, 8))
 LONG_RES_BUFS = 3
 SHORT_RES_BUFS = 4
-TURNED = (2, 4, 6, 8, 9, 10)
+TURNED = (1, 3, 5, 7, 8, 9)
 TURN_LAST = 2
 
 FLOPS = 2 * BINS * SAMPLES * K * C
 
 
 def chunk_list():
-    chunks = [(n, j, CHUNK) for n in range(BINS) for j in range(0, ROWS, CHUNK)]
-    cut = []
-    for index, (n, j, size) in enumerate(chunks):
-        if index == 0:
-            cut.extend([(n, j, size // 2), (n, j + size // 2, size // 2)])
-        else:
-            cut.append((n, j, size))
-    return cut
+    return [(n, j, CHUNK) for n in range(BINS) for j in range(0, ROWS, CHUNK)]
 
 
 def pieces(cuts):
@@ -62,8 +55,8 @@ def tile_gmpahead_pa_t_e_kernel(tc, pooled, p, Wout_words, Wout_scales, out):
         f_pool = ctx.enter_context(tc.tile_pool(name="f", bufs=P_BUFS))
         mx_pool = ctx.enter_context(tc.tile_pool(name="mx", bufs=2))
         work = ctx.enter_context(tc.tile_pool(name="work", bufs=3))
-        t_psum = ctx.enter_context(tc.psum_pool(name="t_psum", bufs=3))
-        y_psum = ctx.enter_context(tc.psum_pool(name="y_psum", bufs=3))
+        t_psum = ctx.enter_context(tc.psum_pool(name="t_psum", bufs=4))
+        y_psum = ctx.enter_context(tc.psum_pool(name="y_psum", bufs=2))
         turn_psum = ctx.enter_context(tc.psum_pool(name="turn_psum", bufs=2))
         ctx.enter_context(tc.manual_schedule())
 

@@ -55,8 +55,8 @@ def tile_gmpahead_pa_t_e_kernel(tc, pooled, p, Wout_words, Wout_scales, out):
         f_pool = ctx.enter_context(tc.tile_pool(name="f", bufs=P_BUFS))
         mx_pool = ctx.enter_context(tc.tile_pool(name="mx", bufs=2))
         work = ctx.enter_context(tc.tile_pool(name="work", bufs=3))
-        t_psum = ctx.enter_context(tc.psum_pool(name="t_psum", bufs=4))
-        y_psum = ctx.enter_context(tc.psum_pool(name="y_psum", bufs=2))
+        t_psum = ctx.enter_context(tc.psum_pool(name="t_psum", bufs=3))
+        y_psum = ctx.enter_context(tc.psum_pool(name="y_psum", bufs=3))
         turn_psum = ctx.enter_context(tc.psum_pool(name="turn_psum", bufs=2))
         ctx.enter_context(tc.manual_schedule())
 

from contextlib import ExitStack

import concourse.mybir as mybir
from concourse.masks import make_identity

F32 = mybir.dt.float32
BF16 = mybir.dt.bfloat16
I32 = mybir.dt.int32
U32 = mybir.dt.uint32
U8 = mybir.dt.uint8
FP8X4 = mybir.dt.float8_e4m3fn_x4
MAX = mybir.AluOpType.max
ADD = mybir.AluOpType.add
RELU = mybir.ActivationFunctionType.Relu

P = 128
BINS = 4
SAMPLES = 3072
K = 512
PACK = 4
FRAMES = 4
C = 128
LEAKY_SLOPE = 0.01

ROWS = SAMPLES // P
CHUNK = 8
PAIR = 2
QUAD = 4
X_BUFS = 5
P_BUFS = 4
AHEAD = 5
P_CUTS = ((8, 16), (8, 16), (8, 16), (8, 16))
OUT_CUTS = ((24,), (24,), (24,), (8, 8, 8))
LONG_RES_BUFS = 3
SHORT_RES_BUFS = 4
TURNED = (1, 3, 5, 7, 8, 9)
TURN_LAST = 2

FLOPS = 2 * BINS * SAMPLES * K * C


def chunk_list():
    return [(n, j, CHUNK) for n in range(BINS) for j in range(0, ROWS, CHUNK)]


def pieces(cuts):
    return [(n, sum(cut[:i]), size) for n, cut in enumerate(cuts) for i, size in enumerate(cut)]


def tile_gmpahead_pa_t_e_kernel(tc, pooled, p, Wout_words, Wout_scales, out):
    nc = tc.nc
    with ExitStack() as ctx:
        const = ctx.enter_context(tc.tile_pool(name="const", bufs=1))
        x_pool = ctx.enter_context(tc.tile_pool(name="x", bufs=X_BUFS))
        f_pool = ctx.enter_context(tc.tile_pool(name="f", bufs=P_BUFS))
        mx_pool = ctx.enter_context(tc.tile_pool(name="mx", bufs=2))
        work = ctx.enter_context(tc.tile_pool(name="work", bufs=3))
        t_psum = ctx.enter_context(tc.psum_pool(name="t_psum", bufs=3))
        y_psum = ctx.enter_context(tc.psum_pool(name="y_psum", bufs=3))
        turn_psum = ctx.enter_context(tc.psum_pool(name="turn_psum", bufs=2))
        ctx.enter_context(tc.manual_schedule())

        chunks = chunk_list()
        n_chunks = len(chunks)
        p_pieces = pieces(P_CUTS)
        out_pieces = pieces(OUT_CUTS)
        x_tiles = {}
        f_tiles = {}
        grouped_tiles = {}
        code_tiles = {}
        y_tiles = {}
        small_tiles = {}
        half_tiles = {}
        top_tiles = {}
        res_tiles = {}
        turned_y = {}
        part_tiles = {}
        leaky_tiles = {}

        def at_end(k):
            return k >= n_chunks - TURN_LAST

        def plain_quads(k):
            size = chunks[k][2]
            if at_end(k):
                return 0
            return size - QUAD if size == CHUNK and k in TURNED else size

        def rows_of(dram, piece):
            n, first, size = piece
            return dram[n].rearrange("(q j) w -> q j w", j=ROWS)[:, first : first + size, :]

        def load_x(k):
            x_tiles[k] = x_pool.tile([P, chunks[k][2], K], BF16, name="x")
            nc.sync.dma_start(out=x_tiles[k][:], in_=rows_of(pooled, chunks[k]))

        def place(k, longer):
            n, first, size = chunks[k]
            for i, (piece_n, piece_first, piece_size) in enumerate(longer):
                if piece_n == n and piece_first <= first < piece_first + piece_size:
                    return i, slice(first - piece_first, first - piece_first + size)

        def load_f(k):
            i, tiles = place(k, p_pieces)
            if tiles.start == 0:
                f_tiles[i] = f_pool.tile([P, p_pieces[i][2], FRAMES * C], BF16, name="f")
                nc.sync.dma_start(out=f_tiles[i][:], in_=rows_of(p.rearrange("n b t c -> n b (t c)"), p_pieces[i]))

        def result(k):
            i, tiles = place(k, out_pieces)
            if i not in res_tiles:
                size = out_pieces[i][2]
                if size > CHUNK:
                    res_tiles[i] = work.tile([P, size, C], F32, name="long_res", bufs=LONG_RES_BUFS)
                else:
                    res_tiles[i] = work.tile([P, size, C], F32, name="short_res", bufs=SHORT_RES_BUFS)
            return res_tiles[i][:, tiles, :]

        def transpose(k):
            size = chunks[k][2]
            words = x_tiles[k][:].bitcast(F32)
            grouped_tiles[k] = mx_pool.tile([P, size, P, PACK], BF16, name="grouped", align_bytes=64)
            grouped_words = grouped_tiles[k][:].bitcast(F32)
            for j in range(0, size, PAIR):
                xt = t_psum.tile([P, PAIR, 2, P], F32, name="xt")
                for i in range(PAIR):
                    for u in range(2):
                        nc.tensor.transpose(xt[:, i, u, :], words[:, j + i, u : K // 2 : 2], ident[:])
                nc.scalar.copy(
                    out=grouped_words[:, j : j + PAIR, :, :],
                    in_=xt[:].rearrange("r i u s -> r i s u"),
                )

        def quantise(k):
            size = chunks[k][2]
            codes = mx_pool.tile([P, size * P], U32, name="codes", align_bytes=64)
            scales = mx_pool.tile([P, size * P], U8, name="scales", align_bytes=64)
            nc.vector.quantize_mx(
                out=codes[:].bitcast(FP8X4),
                scales=scales[:],
                in_=grouped_tiles[k][:].rearrange("r j s t -> r (j s t)"),
            )
            code_tiles[k] = (codes, scales)

        def multiply(k):
            n, first, size = chunks[k]
            codes, scales = code_tiles[k]
            y_tiles[k] = []
            for j in range(0, plain_quads(k), QUAD):
                y = y_psum.tile([P, QUAD, C], F32, name="y")
                for i in range(QUAD):
                    cols = slice((j + i) * P, (j + i + 1) * P)
                    nc.tensor.matmul_mx(
                        out=y[:, i, :],
                        lhsT=codes[:, cols].bitcast(FP8X4),
                        lhsT_scale=scales[:, cols],
                        rhs=w_words[:, n, :].bitcast(FP8X4),
                        rhs_scale=w_scales[:, n, :],
                        start=True,
                        stop=True,
                    )
                y_tiles[k].append(y)
            turned_y[k] = []
            for j in range(plain_quads(k), size, QUAD):
                y = y_psum.tile([P, QUAD * P], F32, name="y")
                cols = slice(j * P, (j + QUAD) * P)
                nc.tensor.matmul_mx(
                    out=y[:],
                    lhsT=w_words[:, n, :].bitcast(FP8X4),
                    lhsT_scale=w_scales[:, n, :],
                    rhs=codes[:, cols].bitcast(FP8X4),
                    rhs_scale=scales[:, cols],
                    start=True,
                    stop=True,
                )
                turned_y[k].append(y)

        def turn_back(k):
            if at_end(k):
                leaky_tiles[k] = []
                for bent, straight in part_tiles[k]:
                    turned_back = t_psum.tile([P, QUAD, C], F32, name="xt")
                    for j in range(QUAD):
                        cols = slice(j * P, (j + 1) * P)
                        nc.tensor.matmul(
                            out=turned_back[:, j, :], lhsT=bent[:, cols], rhs=ident[:], is_transpose=True, start=True, stop=False
                        )
                        nc.tensor.matmul(
                            out=turned_back[:, j, :], lhsT=straight[:, cols], rhs=ident[:], is_transpose=True, start=False, stop=True
                        )
                    leaky_tiles[k].append(turned_back)
                return
            for index, (bent, straight) in enumerate(part_tiles[k]):
                first = plain_quads(k) + index * QUAD
                feat = turn_psum.tile([P, QUAD, C], F32, name="feat")
                nc.tensor.matmul(
                    out=feat[:].rearrange("q j c -> q (j c)"),
                    lhsT=ident_bf[:],
                    rhs=top_tiles[k][:, first : first + QUAD, :].rearrange("q j c -> q (j c)"),
                    start=True,
                    stop=False,
                )
                for j in range(QUAD):
                    cols = slice(j * P, (j + 1) * P)
                    nc.tensor.matmul(
                        out=feat[:, j, :], lhsT=bent[:, cols], rhs=ident[:], is_transpose=True, start=False, stop=False
                    )
                    nc.tensor.matmul(
                        out=feat[:, j, :],
                        lhsT=straight[:, cols],
                        rhs=ident[:],
                        is_transpose=True,
                        start=False,
                        stop=(j == QUAD - 1),
                    )
                nc.scalar.copy(out=result(k)[:, first : first + QUAD, :], in_=feat[:])

        def shrink(k):
            small_tiles[k] = []
            for y in y_tiles[k]:
                small = work.tile([P, QUAD, C], F32, name="small", bufs=4)
                nc.scalar.mul(out=small[:], in_=y[:], mul=LEAKY_SLOPE)
                small_tiles[k].append(small)
            part_tiles[k] = []
            for y in turned_y[k]:
                bent = work.tile([P, QUAD * P], F32, name="bent", bufs=4)
                straight = work.tile([P, QUAD * P], F32, name="straight", bufs=4)
                nc.scalar.activation(out=bent[:], in_=y[:], func=RELU, scale=1.0 - LEAKY_SLOPE)
                nc.scalar.mul(out=straight[:], in_=y[:], mul=LEAKY_SLOPE)
                part_tiles[k].append((bent, straight))

        def leaky(k):
            for h in range(plain_quads(k) // QUAD):
                nc.vector.tensor_tensor(
                    out=result(k)[:, h * QUAD : (h + 1) * QUAD, :],
                    in0=y_tiles[k][h][:],
                    in1=small_tiles[k][h][:],
                    op=MAX,
                )

        def frames_first(k):
            i, tiles = place(k, p_pieces)
            f = f_tiles[i][:, tiles, :].rearrange("q j (t c) -> q j t c", t=FRAMES)
            half_tiles[k] = work.tile([P, chunks[k][2], 2, C], BF16, name="half", bufs=2)
            nc.vector.tensor_tensor(out=half_tiles[k][:], in0=f[:, :, 0:2, :], in1=f[:, :, 2:4, :], op=MAX)

        def frames_second(k):
            half = half_tiles[k]
            top_tiles[k] = work.tile([P, chunks[k][2], C], BF16, name="top", bufs=4)
            nc.vector.tensor_tensor(out=top_tiles[k][:], in0=half[:, :, 0, :], in1=half[:, :, 1, :], op=MAX)

        def finish(k):
            mine = slice(0, plain_quads(k))
            for index, turned_back in enumerate(leaky_tiles.get(k, [])):
                quad = slice(index * QUAD, (index + 1) * QUAD)
                nc.vector.tensor_tensor(
                    out=result(k)[:, quad, :], in0=turned_back[:], in1=top_tiles[k][:, quad, :], op=ADD
                )
            if plain_quads(k) > 0:
                nc.vector.tensor_tensor(
                    out=result(k)[:, mine, :], in0=result(k)[:, mine, :], in1=top_tiles[k][:, mine, :], op=ADD
                )
            i, tiles = place(k, out_pieces)
            if tiles.stop == out_pieces[i][2]:
                nc.sync.dma_start(out=rows_of(out, out_pieces[i]), in_=res_tiles[i][:])

        ident = const.tile([P, P], F32, name="ident")
        make_identity(nc, ident[:])
        ident_bf = const.tile([P, P], BF16, name="ident_bf")
        make_identity(nc, ident_bf[:])
        w_words = const.tile([P, BINS, C * PACK], U8, name="w_words", align_bytes=64)
        w_scales = const.tile([P, BINS, C], U8, name="w_scales", align_bytes=64)
        nc.vector.memset(w_scales[:].bitcast(I32), 0)

        load_x(0)
        nc.sync.dma_start(
            out=w_words[:].bitcast(I32),
            in_=Wout_words.rearrange("g r c t -> r g (c t)").bitcast(I32),
        )
        for quadrant in range(4):
            nc.sync.dma_start(
                out=w_scales[32 * quadrant : 32 * quadrant + 4].bitcast(I32),
                in_=Wout_scales[:, 4 * quadrant : 4 * quadrant + 4, :].rearrange("g q c -> q g c").bitcast(I32),
            )
        for k in range(1, AHEAD):
            load_x(k)
            if k >= 2:
                load_f(k - 2)

        for k in range(n_chunks + 3):
            if k + AHEAD < n_chunks:
                load_x(k + AHEAD)
            if k + AHEAD - 2 < n_chunks:
                load_f(k + AHEAD - 2)
            if k < n_chunks:
                transpose(k)
            if 2 <= k <= n_chunks + 1:
                leaky(k - 2)
            if 1 <= k <= n_chunks:
                multiply(k - 1)
                shrink(k - 1)
            if k >= 3 and not at_end(k - 3):
                turn_back(k - 3)
            if 2 <= k <= n_chunks + 1 and at_end(k - 2):
                turn_back(k - 2)
            if 2 <= k <= n_chunks + 1:
                frames_first(k - 2)
            if k >= 3:
                finish(k - 3)
            if 2 <= k <= n_chunks + 1:
                frames_second(k - 2)
            if k < n_chunks:
                quantise(k)
